import numpy as np
import ml_dtypes


def mxq(x, axis, fmt="e4m3"):
    dtype, down = {"e4m3": (ml_dtypes.float8_e4m3fn, 7), "e5m2": (ml_dtypes.float8_e5m2, 14)}[fmt]
    v = np.moveaxis(np.asarray(x, np.float32).astype(ml_dtypes.bfloat16).astype(np.float64), axis, -1)
    blocks = v.reshape(v.shape[:-1] + (-1, 32))
    amax = np.abs(blocks).max(-1, keepdims=True)
    byte = np.maximum(np.where(amax > 0, np.frexp(amax)[1] - 1 + 127, 0) - down, 1)
    scale = np.exp2(byte - 127.0)
    codes = (blocks / scale).astype(np.float32).astype(dtype).astype(np.float64)
    return np.moveaxis((codes * scale).reshape(v.shape), -1, axis)


WIDE = False


def mx_kscale(k):
    if not WIDE:
        return np.ones(k)
    levels = np.array([10, -10, 5, -5, 0])
    a = np.random.permutation(np.resize(levels, k // 512 * 4)).reshape(k // 512, 4)
    idx = np.arange(k)
    return np.exp2(a[idx // 512, idx % 128 // 32])


BF16 = ml_dtypes.bfloat16


def bf(x):
    return np.asarray(x, np.float32).astype(BF16)


def f64(x):
    return np.asarray(x).astype(np.float64)


B, D0, D1, D2, D3 = 512, 2048, 2048, 2048, 2048
HEBB = 0.01
RATE = 0.001
BATCH_NUM = 1
C = HEBB * RATE / BATCH_NUM


def centred(s):
    return s / np.exp2(np.round(np.log2(s.mean())))


def setup_inputs():
    s, t = centred(mx_kscale(D0)), centred(mx_kscale(D1))
    return {"x": bf((4.0 + 3.0 * np.random.standard_normal((B, D0))) * s),
            "W1": bf(np.random.standard_normal((D1, D0)) * 0.9 / np.sqrt(D0) / s[None, :] * t[:, None]),
            "b1": bf((3.0 + 1.5 * np.random.standard_normal(D1)) * t),
            "W2": bf(np.random.standard_normal((D2, D1)) * 0.9 / np.sqrt(D1) / t[None, :]),
            "b2": bf(3.0 + 1.5 * np.random.standard_normal(D2))}


def reference(x, W1, b1, W2, b2):
    x = f64(x)
    v1 = np.maximum((mxq(x, 1, "e4m3") @ mxq(f64(W1), 1, "e4m3").T) + f64(b1), 0.0)
    m1 = np.mean(v1, axis=0)
    h = v1 + np.sum(x, axis=1, keepdims=True) * (C * m1)[None, :]
    v2 = np.maximum((mxq(h, 1, "e4m3") @ mxq(f64(W2), 1, "e4m3").T) + f64(b2), 0.0)
    m2 = np.mean(v2, axis=0)
    out = v2 + np.sum(h, axis=1, keepdims=True) * (C * m2)[None, :]
    return out, m1, m2

@@ -1,0 +1,370 @@
+from contextlib import ExitStack
+
+import concourse.mybir as mybir
+from concourse.masks import make_identity
+
+F32 = mybir.dt.float32
+BF16 = mybir.dt.bfloat16
+U32 = mybir.dt.uint32
+U8 = mybir.dt.uint8
+FP8X4 = mybir.dt.float8_e4m3fn_x4
+ACT = mybir.ActivationFunctionType
+ALU = mybir.AluOpType
+AX = mybir.AxisListType
+
+P = 128
+ROWS = 512
+C = 0.01 * 0.001 / 1
+FLOPS = 2 * 2 * 512 * 2048 * 2048
+
+NW = 6
+EW_ENG = ["SSSS", "SSSV"]
+EW0_ENG = "SVSV"
+LAG = 2
+ADDS_L1 = 1
+ADDS_L2 = 4
+TO_PER_STEP = 2
+SH_DELAY = 3
+REP_ENG = "G"
+NV = 12
+
+
+def tile_optimalnet_pa_kernel(tc, x, W1, b1, W2, b2, out_0, out_1, out_2):
+    nc = tc.nc
+    with ExitStack() as ctx:
+        const = ctx.enter_context(tc.tile_pool(name="const", bufs=1))
+        win = ctx.enter_context(tc.tile_pool(name="win", bufs=NW))
+        stage = ctx.enter_context(tc.tile_pool(name="stage", bufs=3))
+        work = ctx.enter_context(tc.tile_pool(name="work", bufs=2))
+        psT = ctx.enter_context(tc.psum_pool(name="psT", bufs=6))
+        psM = ctx.enter_context(tc.psum_pool(name="psM", bufs=2))
+        ctx.enter_context(tc.manual_schedule())
+
+        def copy_on(eng, out, in_):
+            if eng == "V":
+                nc.vector.tensor_copy(out=out, in_=in_)
+            else:
+                nc.scalar.copy(out=out, in_=in_)
+
+        bz = const.tile([P, 256], BF16, name="bz")
+        nc.vector.memset(bz[:], 0.0)
+        nc.sync.dma_start(out=bz[0:8, :], in_=b1.rearrange("(c n) -> c n", n=256))
+        nc.sync.dma_start(out=bz[8:16, :], in_=b2.rearrange("(c n) -> c n", n=256))
+        xt = [win.tile([P, 4096], BF16, name="x0", tag="w"), win.tile([P, 4096], BF16, name="x1", tag="w")]
+        w0 = win.tile([P, 4096], BF16, name="w0", tag="w")
+
+        def load_x(rt):
+            nc.sync.dma_start(out=xt[rt // 2][:, (rt % 2) * 2048:(rt % 2 + 1) * 2048], in_=x[rt * P:(rt + 1) * P, :])
+
+        def load_w0(e):
+            nc.sync.dma_start(out=w0[:, e * 2048:(e + 1) * 2048], in_=W1.rearrange("(c p e) k -> c p e k", p=P, e=2)[0][:, e, :])
+
+        load_x(0)
+        load_x(1)
+        load_x(2)
+        load_w0(0)
+        load_x(3)
+        load_w0(1)
+        ident = const.tile([P, P], F32, name="ident")
+        make_identity(nc, ident[:])
+        ones_b = const.tile([P, P], BF16, name="ones_b")
+        nc.vector.memset(ones_b[:], 1.0)
+        ones_f = const.tile([P, P], F32, name="ones_f")
+        nc.vector.memset(ones_f[:], 1.0)
+        mp = [const.tile([P, 256], F32, name="mp0"), const.tile([P, 16], F32, name="mp1")]
+        nc.vector.memset(mp[0][:], 0.0)
+
+        gx = const.tile([P, 8192], BF16, name="gx", align_bytes=64)
+        xc = const.tile([P, 2048], U32, name="xc", align_bytes=64)
+        xsc = const.tile([P, 2048], U8, name="xsc", align_bytes=64)
+        hc = const.tile([P, 2048], U32, name="hc", align_bytes=64)
+        hsc = const.tile([P, 2048], U8, name="hsc", align_bytes=64)
+        bw = const.tile([P, 16], F32, name="bw")
+        biasf = const.tile([P, 32], F32, name="biasf")
+        sxr = const.tile([P, ROWS], F32, name="sxr")
+        sxc = const.tile([P, ROWS], F32, name="sxc")
+        acc = const.tile([P, ROWS], F32, name="acc")
+        accf = const.tile([P, ROWS], F32, name="accf")
+        shc = const.tile([P, 4], F32, name="shc")
+        s1 = const.tile([P, 1], F32, name="s1")
+        m2b = const.tile([P, 2048], F32, name="m2b")
+
+        wsrc = [W1.rearrange("(c p e) k -> c p (e k)", p=P, e=2), W2.rearrange("(c p e) k -> c p (e k)", p=P, e=2)]
+        wt, tb, gw, wc, ws, mb, vt, ob, hcn, gh, rep = {}, {}, {}, {}, {}, {}, {}, {}, {}, {}, {}
+
+        def load(b):
+            t = win.tile([P, 4096], BF16, name="w%d" % b, tag="w")
+            nc.sync.dma_start(out=t[:], in_=wsrc[b // 8][b % 8])
+            wt[b] = t
+
+        def four_transposes(bank, src32, cols):
+            for i in range(4):
+                nc.tensor.transpose(out=bank[:, i * P:(i + 1) * P], in_=src32[:, cols[i]:cols[i] + P], identity=ident[:])
+
+        def tx(rt):
+            x32 = xt[rt // 2][:].bitcast(F32)
+            for gp in range(2):
+                bank = psT.tile([P, 512], F32, name="tx%d_%d" % (rt, gp), tag="T")
+                four_transposes(bank, x32, [(rt % 2) * 1024 + (2 * gp + gl) * 256 + u * P for gl in range(2) for u in range(2)])
+                tb[("x", rt, gp)] = bank
+
+        def ex(rt, gp, eng):
+            dst = gx[:].bitcast(F32).rearrange("p (g r u) -> p g r u", g=4, u=2)[:, 2 * gp:2 * gp + 2, rt * P:(rt + 1) * P, :]
+            copy_on(eng, dst, tb[("x", rt, gp)][:].rearrange("p (g u r) -> p g r u", g=2, u=2))
+
+        def qx(rt):
+            for g in range(4):
+                lo = g * 512 + rt * P
+                nc.vector.quantize_mx(out=xc[:, lo:lo + P].bitcast(FP8X4), scales=xsc[:, lo:lo + P], in_=gx[:, 4 * lo:4 * (lo + P)])
+
+        def sxmm(rt):
+            bank = psT.tile([P, 512], F32, name="sx%d" % rt, tag="T")
+            for g in range(4):
+                nc.tensor.matmul(out=bank[:], lhsT=ones_b[:], rhs=gx[:, g * 2048 + rt * 512:g * 2048 + (rt + 1) * 512],
+                                 start=(g == 0), stop=(g == 3))
+            tb[("s", rt)] = bank
+
+        def rsx(rt):
+            nc.vector.tensor_reduce(out=sxr[:, rt * P:(rt + 1) * P], in_=tb[("s", rt)][:].rearrange("p (r t) -> p r t", t=4),
+                                    axis=AX.X, op=ALU.add)
+
+        def tw(b, which=(0, 1, 2, 3)):
+            w32 = wt[b][:].bitcast(F32)
+            for i in which:
+                e, gp = i // 2, i % 2
+                bank = psT.tile([P, 512], F32, name="tw%d_%d" % (b, i), tag="T")
+                four_transposes(bank, w32, [e * 1024 + (2 * gp + gl) * 256 + u * P for gl in range(2) for u in range(2)])
+                tb[(b, i)] = bank
+
+        def ew(b, i, eng):
+            if i == 0:
+                gw[b] = stage.tile([P, 4096], BF16, name="gw%d" % b, tag="gw", align_bytes=64)
+            dst = gw[b][:].bitcast(F32)[:, i * 512:(i + 1) * 512].rearrange("p (g o u) -> p g o u", g=2, u=2)
+            copy_on(eng, dst, tb[(b, i)][:].rearrange("p (g u o) -> p g o u", g=2, u=2))
+
+        def qw(b, half=None):
+            if half != 1:
+                wc[b] = stage.tile([P, 1024], U32, name="wc%d" % b, tag="wc", align_bytes=64)
+                ws[b] = stage.tile([P, 1024], U8, name="ws%d" % b, tag="ws", align_bytes=64)
+            if half is None:
+                nc.vector.quantize_mx(out=wc[b][:].bitcast(FP8X4), scales=ws[b][:], in_=gw[b][:])
+            else:
+                lo = half * 512
+                nc.vector.quantize_mx(out=wc[b][:, lo:lo + 512].bitcast(FP8X4), scales=ws[b][:, lo:lo + 512], in_=gw[b][:, 4 * lo:4 * lo + 2048])
+
+        def mm(b, es=(0, 1), gs=(0, 1, 2, 3)):
+            rc, rs = (xc, xsc) if b < 8 else (hc, hsc)
+            for e in es:
+                if gs[0] == 0:
+                    mb[(b, e)] = psM.tile([P, 512], F32, name="m%d_%d" % (b, e), tag="M")
+            seq = [(e, g) for e in es for g in gs]
+            for e, g in seq:
+                lo = (e * 4 + g) * P
+                nc.tensor.matmul_mx(out=mb[(b, e)][:], lhsT=wc[b][:, lo:lo + P].bitcast(FP8X4), lhsT_scale=ws[b][:, lo:lo + P],
+                                    rhs=rc[:, g * 512:(g + 1) * 512].bitcast(FP8X4), rhs_scale=rs[:, g * 512:(g + 1) * 512],
+                                    start=(g == 0), stop=(g == 3))
+
+        def msum(b, e):
+            col = e * P + b if b < 8 else (b - 8) * 2 + e
+            return mp[b // 8][:, col:col + 1]
+
+        def act(b, e):
+            j = (b // 8) * 16 + (b % 8) * 2 + e
+            vt[(b, e)] = work.tile([P, ROWS], F32, name="v%d_%d" % (b, e), tag="v", bufs=NV)
+            nc.scalar.activation(out=vt[(b, e)][:], in_=mb[(b, e)][:], func=ACT.Relu, bias=biasf[:, j:j + 1], scale=1.0,
+                                 accum_out=msum(b, e))
+            if b >= 8:
+                rep[(b, e)] = work.tile([P, P], F32, name="rep%d_%d" % (b, e), tag="rep", bufs=NV)
+                if REP_ENG == "G" and b < 14:
+                    nc.gpsimd.tensor_scalar(out=rep[(b, e)][:], in0=ones_f[:], scalar1=msum(b, e), scalar2=1.0 / ROWS, op0=ALU.mult, op1=ALU.mult)
+                else:
+                    nc.vector.tensor_scalar(out=rep[(b, e)][:], in0=ones_f[:], scalar1=msum(b, e), scalar2=1.0 / ROWS, op0=ALU.mult, op1=ALU.mult)
+
+        pending = []
+        added = [0]
+
+        def hh(b, e):
+            g, t = b // 2, 2 * (b % 2) + e
+            if t == 0:
+                hcn[g] = work.tile([P, 2048], BF16, name="hcn%d" % g, tag="hcn")
+            nc.vector.scalar_tensor_tensor(out=hcn[g][:, t * ROWS:(t + 1) * ROWS], in0=sxc[:], scalar=msum(b, e), in1=vt[(b, e)][:],
+                                           op0=ALU.mult, op1=ALU.add)
+            pending.append((b, e))
+
+        def adds(n):
+            for i in range(n):
+                if added[0] == 0 and len(pending) >= 2:
+                    nc.vector.tensor_tensor(out=acc[:], in0=vt[pending[0]][:], in1=vt[pending[1]][:], op=ALU.add)
+                    added[0] = 2
+                elif 0 < added[0] < len(pending):
+                    nc.vector.tensor_tensor(out=acc[:], in0=acc[:], in1=vt[pending[added[0]]][:], op=ALU.add)
+                    added[0] = added[0] + 1
+
+        def rg(g):
+            gh[g] = work.tile([P, 2048], BF16, name="gh%d" % g, tag="gh", align_bytes=64)
+            nc.vector.tensor_copy(out=gh[g][:].rearrange("p (c i t) -> p c t i", i=4, t=4),
+                                  in_=hcn[g][:].rearrange("p (t c i) -> p c t i", t=4, i=4))
+
+        def qh(g):
+            nc.vector.quantize_mx(out=hc[:, g * 512:(g + 1) * 512].bitcast(FP8X4), scales=hsc[:, g * 512:(g + 1) * 512], in_=gh[g][:])
+
+        def sh_vector():
+            nc.vector.tensor_reduce(out=s1[:], in_=mp[0][:], axis=AX.X, op=ALU.add)
+            nc.vector.scalar_tensor_tensor(out=accf[:], in0=sxc[:], scalar=s1[:], in1=acc[:], op0=ALU.mult, op1=ALU.add)
+
+        def sh_rest():
+            bank = psT.tile([P, 512], F32, name="shb", tag="T")
+            for rb in range(4):
+                nc.tensor.matmul(out=bank[:, rb * 32:(rb + 1) * 32], lhsT=accf[:, rb * P:(rb + 1) * P], rhs=ones_f[:, 0:32], start=True, stop=True)
+            nc.scalar.mul(out=shc[:], in_=bank[:, 0:P].rearrange("p (b n) -> p b n", n=32)[:, :, 0], mul=C)
+
+        def to(b):
+            for k in range(2):
+                bank = psT.tile([P, 512], F32, name="to%d_%d" % (b, k), tag="T")
+                for l in range(2):
+                    for e in range(2):
+                        rb = 2 * k + l
+                        nc.tensor.transpose(out=bank[:, (l * 2 + e) * P:(l * 2 + e + 1) * P], in_=vt[(b, e)][:, rb * P:(rb + 1) * P],
+                                            identity=ident[:])
+                tb[("o", b, k)] = bank
+            bank = psT.tile([P, 512], F32, name="tr%d" % b, tag="T")
+            for e in range(2):
+                nc.tensor.transpose(out=bank[:, e * P:(e + 1) * P], in_=rep[(b, e)][:], identity=ident[:])
+            tb[("r", b)] = bank
+
+        def em(b):
+            c = b - 8
+            nc.scalar.copy(out=m2b[:, c * 256:(c + 1) * 256].rearrange("r (p e) -> r p e", e=2),
+                           in_=tb[("r", b)][:, 0:256].rearrange("r (e p) -> r p e", e=2))
+
+        def eo(b):
+            c = b - 8
+            ob[b] = work.tile([P, 1024], F32, name="o%d" % b, tag="o", bufs=3)
+            for rb in range(4):
+                k, l = rb // 2, rb % 2
+                nc.vector.scalar_tensor_tensor(out=ob[b][:, rb * 256:(rb + 1) * 256].rearrange("r (p e) -> r p e", e=2),
+                                               in0=m2b[:, c * 256:(c + 1) * 256].rearrange("r (p e) -> r p e", e=2),
+                                               scalar=shc[:, rb:rb + 1],
+                                               in1=tb[("o", b, k)][:, l * 256:(l + 1) * 256].rearrange("r (e p) -> r p e", e=2),
+                                               op0=ALU.mult, op1=ALU.add)
+                if b == 15 and rb % 2 == 1:
+                    nc.sync.dma_start(out=out_0.rearrange("(k r) o -> r k o", r=P)[:, rb - 1:rb + 1, c * 256:(c + 1) * 256],
+                                      in_=ob[b][:].rearrange("r (k o) -> r k o", k=4)[:, rb - 1:rb + 1, :])
+            if b < 15:
+                nc.sync.dma_start(out=out_0.rearrange("(k r) o -> r k o", r=P)[:, :, c * 256:(c + 1) * 256],
+                                  in_=ob[b][:].rearrange("r (k o) -> r k o", k=4))
+
+        def mout1():
+            bank = psT.tile([P, 512], F32, name="mo", tag="T")
+            for e in range(2):
+                nc.tensor.transpose(out=bank[:, e * P:(e + 1) * P], in_=mp[0][:, e * P:(e + 1) * P], identity=ident[:])
+            ms = work.tile([P, 256], F32, name="ms", tag="ms", bufs=1)
+            nc.scalar.activation(out=ms[:].rearrange("c (p e) -> c p e", e=2), in_=bank[:, 0:256].rearrange("c (e p) -> c p e", e=2),
+                                 func=ACT.Copy, scale=1.0 / ROWS)
+            nc.sync.dma_start(out=out_1.rearrange("(c n) -> c n", n=256), in_=ms[0:8, :])
+
+        wt[0] = w0
+        for b in range(1, NW - 2):
+            load(b)
+        bank = psT.tile([P, 512], F32, name="tbias", tag="T")
+        nc.tensor.transpose(out=bank[:, 0:P], in_=bz[:].bitcast(F32), identity=ident[:])
+        nc.vector.tensor_copy(out=bw[:], in_=bank[:, 0:16])
+        nc.vector.tensor_copy(out=biasf[:], in_=bw[:].bitcast(BF16))
+
+        def txe(rt):
+            tx(rt)
+            ex(rt, 0, "V")
+            ex(rt, 1, "S")
+            qx(rt)
+
+        txe(0)
+        txe(1)
+        load(NW - 2)
+        sxmm(0)
+        rsx(0)
+        txe(2)
+        tw(0, (0, 1))
+        ew(0, 0, "S")
+        ew(0, 1, "V")
+        qw(0, 0)
+        txe(3)
+        load(NW - 1)
+        sxmm(1)
+        tw(0, (2, 3))
+        load(NW)
+        ew(0, 2, "S")
+        ew(0, 3, "V")
+        qw(0, 1)
+        rsx(1)
+
+        sh_step = [99]
+        turned = [8]
+        for b in range(18):
+            prev = b - 1
+            tnext = b + 1 if b <= 8 else b + 2
+            if b == 0:
+                mm(0, (0,))
+            if tnext <= 15:
+                tw(tnext)
+                if tnext + NW <= 15:
+                    load(tnext + NW)
+            if 0 <= prev <= 15:
+                act(prev, 1)
+                if prev <= 7:
+                    hh(prev, 1)
+                    if prev % 2 == 1:
+                        rg(prev // 2)
+                    if prev == 7:
+                        qh(3)
+                    else:
+                        adds(ADDS_L1)
+            if tnext <= 15:
+                for i in range(4):
+                    ew(tnext, i, EW_ENG[tnext // 8][i])
+            if b == sh_step[0] + SH_DELAY:
+                sh_rest()
+            if b >= sh_step[0] + SH_DELAY:
+                for i in range(TO_PER_STEP):
+                    if turned[0] <= min(15, b - (LAG if b < 14 else 1)):
+                        to(turned[0])
+                        em(turned[0])
+                        if turned[0] == 15:
+                            nc.sync.dma_start(out=out_2.rearrange("(a n) -> a n", a=1), in_=m2b[0:1, :])
+                        eo(turned[0])
+                        turned[0] = turned[0] + 1
+            if b == 9:
+                mout1()
+            if b == 0:
+                act(0, 0)
+                mm(0, (1,))
+                sxmm(2)
+                sxmm(3)
+            elif b == 8:
+                mm(8, (0, 1), (0, 1, 2))
+                tw(10)
+                if 10 + NW <= 15:
+                    load(10 + NW)
+                for i in range(4):
+                    ew(10, i, "SSSS"[i])
+                mm(8, (0, 1), (3,))
+                act(8, 0)
+            elif b <= 15:
+                mm(b)
+                act(b, 0)
+            if tnext <= 15:
+                qw(tnext)
+            if b == 8:
+                qw(10)
+            if prev % 2 == 1 and 0 < prev < 7:
+                qh(prev // 2)
+            if b == 0:
+                rsx(2)
+                rsx(3)
+                nc.vector.tensor_scalar(out=sxc[:], in0=sxr[:], scalar1=C / ROWS, scalar2=None, op0=ALU.mult)
+            if b <= 7:
+                hh(b, 0)
+            if b >= 8 and sh_step[0] == 99:
+                adds(ADDS_L2)
+                if added[0] == 16:
+                    sh_vector()
+                    sh_step[0] = b

@@ -18,15 +18,18 @@ C = 0.01 * 0.001 / 1
 FLOPS = 2 * 2 * 512 * 2048 * 2048
 
 NW = 6
-EW_ENG = ["SSSS", "SSSV"]
+EW_ENG = ["SSSS", "SSSS"]
 EW0_ENG = "SVSV"
 LAG = 2
-ADDS_L1 = 1
-ADDS_L2 = 4
+ADDS_L1 = 0
+ADDS_L2 = 5
 TO_PER_STEP = 2
 SH_DELAY = 3
 REP_ENG = "G"
-NV = 12
+NV = 18
+WARM0 = 4
+WARM1 = 2
+AH = [1, 1, 1, 1, 1, 1, 1, 1, 1, 2]
 
 
 def tile_optimalnet_pa_kernel(tc, x, W1, b1, W2, b2, out_0, out_1, out_2):
@@ -46,20 +49,23 @@ def tile_optimalnet_pa_kernel(tc, x, W1, b1, W2, b2, out_0, out_1, out_2):
             else:
                 nc.scalar.copy(out=out, in_=in_)
 
-        bz = const.tile([P, 256], BF16, name="bz")
-        nc.vector.memset(bz[:], 0.0)
-        nc.sync.dma_start(out=bz[0:8, :], in_=b1.rearrange("(c n) -> c n", n=256))
-        nc.sync.dma_start(out=bz[8:16, :], in_=b2.rearrange("(c n) -> c n", n=256))
         xt = [win.tile([P, 4096], BF16, name="x0", tag="w"), win.tile([P, 4096], BF16, name="x1", tag="w")]
         w0 = win.tile([P, 4096], BF16, name="w0", tag="w")
 
-        def load_x(rt):
-            nc.sync.dma_start(out=xt[rt // 2][:, (rt % 2) * 2048:(rt % 2 + 1) * 2048], in_=x[rt * P:(rt + 1) * P, :])
+        def load_x(rt, lo=0, hi=2048):
+            nc.sync.dma_start(out=xt[rt // 2][:, (rt % 2) * 2048 + lo:(rt % 2) * 2048 + hi], in_=x[rt * P:(rt + 1) * P, lo:hi])
 
         def load_w0(e):
             nc.sync.dma_start(out=w0[:, e * 2048:(e + 1) * 2048], in_=W1.rearrange("(c p e) k -> c p e k", p=P, e=2)[0][:, e, :])
 
-        load_x(0)
+        load_x(0, 0, 1024)
+        load_x(0, 1024, 2048)
+        ones_b = const.tile([P, 512], BF16, name="ones_b")
+        nc.vector.memset(ones_b[:], 1.0)
+        bz = const.tile([P, 256], BF16, name="bz")
+        nc.vector.memset(bz[:], 0.0)
+        nc.sync.dma_start(out=bz[0:8, :], in_=b1.rearrange("(c n) -> c n", n=256))
+        nc.sync.dma_start(out=bz[8:16, :], in_=b2.rearrange("(c n) -> c n", n=256))
         load_x(1)
         load_x(2)
         load_w0(0)
@@ -67,12 +73,19 @@ def tile_optimalnet_pa_kernel(tc, x, W1, b1, W2, b2, out_0, out_1, out_2):
         load_w0(1)
         ident = const.tile([P, P], F32, name="ident")
         make_identity(nc, ident[:])
-        ones_b = const.tile([P, P], BF16, name="ones_b")
-        nc.vector.memset(ones_b[:], 1.0)
         ones_f = const.tile([P, P], F32, name="ones_f")
         nc.vector.memset(ones_f[:], 1.0)
         mp = [const.tile([P, 256], F32, name="mp0"), const.tile([P, 16], F32, name="mp1")]
         nc.vector.memset(mp[0][:], 0.0)
+        tabl = const.tile([P, 1], F32, name="tabl")
+        nc.scalar.activation(out=tabl[:], in_=ones_f[:, 0:1], func=ACT.Relu)
+        warm = psT.tile([P, 512], F32, name="warm", tag="T")
+
+        def warm_up(n):
+            for i in range(n):
+                nc.tensor.matmul(out=warm[:], lhsT=ones_b[:, 0:P], rhs=ones_b[:], start=True, stop=True)
+
+        warm_up(WARM0)
 
         gx = const.tile([P, 8192], BF16, name="gx", align_bytes=64)
         xc = const.tile([P, 2048], U32, name="xc", align_bytes=64)
@@ -120,7 +133,7 @@ def tile_optimalnet_pa_kernel(tc, x, W1, b1, W2, b2, out_0, out_1, out_2):
         def sxmm(rt):
             bank = psT.tile([P, 512], F32, name="sx%d" % rt, tag="T")
             for g in range(4):
-                nc.tensor.matmul(out=bank[:], lhsT=ones_b[:], rhs=gx[:, g * 2048 + rt * 512:g * 2048 + (rt + 1) * 512],
+                nc.tensor.matmul(out=bank[:], lhsT=ones_b[:, 0:P], rhs=gx[:, g * 2048 + rt * 512:g * 2048 + (rt + 1) * 512],
                                  start=(g == 0), stop=(g == 3))
             tb[("s", rt)] = bank
 
@@ -174,7 +187,7 @@ def tile_optimalnet_pa_kernel(tc, x, W1, b1, W2, b2, out_0, out_1, out_2):
             nc.scalar.activation(out=vt[(b, e)][:], in_=mb[(b, e)][:], func=ACT.Relu, bias=biasf[:, j:j + 1], scale=1.0,
                                  accum_out=msum(b, e))
             if b >= 8:
-                rep[(b, e)] = work.tile([P, P], F32, name="rep%d_%d" % (b, e), tag="rep", bufs=NV)
+                rep[(b, e)] = work.tile([P, P], F32, name="rep%d_%d" % (b, e), tag="rep", bufs=10)
                 if REP_ENG == "G" and b < 14:
                     nc.gpsimd.tensor_scalar(out=rep[(b, e)][:], in0=ones_f[:], scalar1=msum(b, e), scalar2=1.0 / ROWS, op0=ALU.mult, op1=ALU.mult)
                 else:
@@ -266,10 +279,6 @@ def tile_optimalnet_pa_kernel(tc, x, W1, b1, W2, b2, out_0, out_1, out_2):
         wt[0] = w0
         for b in range(1, NW - 2):
             load(b)
-        bank = psT.tile([P, 512], F32, name="tbias", tag="T")
-        nc.tensor.transpose(out=bank[:, 0:P], in_=bz[:].bitcast(F32), identity=ident[:])
-        nc.vector.tensor_copy(out=bw[:], in_=bank[:, 0:16])
-        nc.vector.tensor_copy(out=biasf[:], in_=bw[:].bitcast(BF16))
 
         def txe(rt):
             tx(rt)
@@ -278,6 +287,11 @@ def tile_optimalnet_pa_kernel(tc, x, W1, b1, W2, b2, out_0, out_1, out_2):
             qx(rt)
 
         txe(0)
+        warm_up(WARM1)
+        bank = psT.tile([P, 512], F32, name="tbias", tag="T")
+        nc.tensor.transpose(out=bank[:, 0:P], in_=bz[:].bitcast(F32), identity=ident[:])
+        nc.vector.tensor_copy(out=bw[:], in_=bank[:, 0:16])
+        nc.vector.tensor_copy(out=biasf[:], in_=bw[:].bitcast(BF16))
         txe(1)
         load(NW - 2)
         sxmm(0)
@@ -298,16 +312,21 @@ def tile_optimalnet_pa_kernel(tc, x, W1, b1, W2, b2, out_0, out_1, out_2):
         rsx(1)
 
         sh_step = [99]
+        twd = [0]
         turned = [8]
         for b in range(18):
             prev = b - 1
-            tnext = b + 1 if b <= 8 else b + 2
+            tlist = [t for t in range(twd[0] + 1, min(15, b + AH[min(b, 9)]) + 1)]
             if b == 0:
                 mm(0, (0,))
-            if tnext <= 15:
-                tw(tnext)
-                if tnext + NW <= 15:
-                    load(tnext + NW)
+            for t in tlist:
+                tw(t)
+                twd[0] = t
+                if t + NW <= 15:
+                    load(t + NW)
+                if t != tlist[-1]:
+                    for i in range(4):
+                        ew(t, i, "SVSV"[i])
             if 0 <= prev <= 15:
                 act(prev, 1)
                 if prev <= 7:
@@ -318,9 +337,9 @@ def tile_optimalnet_pa_kernel(tc, x, W1, b1, W2, b2, out_0, out_1, out_2):
                         qh(3)
                     else:
                         adds(ADDS_L1)
-            if tnext <= 15:
+            if len(tlist) > 0:
                 for i in range(4):
-                    ew(tnext, i, EW_ENG[tnext // 8][i])
+                    ew(tlist[-1], i, EW_ENG[tlist[-1] // 8][i])
             if b == sh_step[0] + SH_DELAY:
                 sh_rest()
             if b >= sh_step[0] + SH_DELAY:
@@ -341,20 +360,21 @@ def tile_optimalnet_pa_kernel(tc, x, W1, b1, W2, b2, out_0, out_1, out_2):
                 sxmm(3)
             elif b == 8:
                 mm(8, (0, 1), (0, 1, 2))
-                tw(10)
-                if 10 + NW <= 15:
-                    load(10 + NW)
+                tx_ = twd[0] + 1
+                tw(tx_)
+                twd[0] = tx_
+                if tx_ + NW <= 15:
+                    load(tx_ + NW)
                 for i in range(4):
-                    ew(10, i, "SSSS"[i])
+                    ew(tx_, i, "SSSS"[i])
+                tlist.append(tx_)
                 mm(8, (0, 1), (3,))
                 act(8, 0)
             elif b <= 15:
                 mm(b)
                 act(b, 0)
-            if tnext <= 15:
-                qw(tnext)
-            if b == 8:
-                qw(10)
+            for t in tlist:
+                qw(t)
             if prev % 2 == 1 and 0 < prev < 7:
                 qh(prev // 2)
             if b == 0:

@@ -20,9 +20,9 @@ FLOPS = 2 * 2 * 512 * 2048 * 2048
 NW = 6
 EW_ENG = ["SSSS", "SSSS"]
 EW0_ENG = "SVSV"
-LAG = 2
-ADDS_L1 = 0
 ADDS_L2 = 5
+ADDS_8 = 3
+LAG = 2
 TO_PER_STEP = 2
 SH_DELAY = 3
 REP_ENG = "G"
@@ -96,7 +96,7 @@ def tile_optimalnet_pa_kernel(tc, x, W1, b1, W2, b2, out_0, out_1, out_2):
         biasf = const.tile([P, 32], F32, name="biasf")
         sxr = const.tile([P, ROWS], F32, name="sxr")
         sxc = const.tile([P, ROWS], F32, name="sxc")
-        acc = const.tile([P, ROWS], F32, name="acc")
+        acc = [const.tile([P, ROWS], F32, name="acc0"), const.tile([P, ROWS], F32, name="acc1")]
         accf = const.tile([P, ROWS], F32, name="accf")
         shc = const.tile([P, 4], F32, name="shc")
         s1 = const.tile([P, 1], F32, name="s1")
@@ -187,7 +187,7 @@ def tile_optimalnet_pa_kernel(tc, x, W1, b1, W2, b2, out_0, out_1, out_2):
             nc.scalar.activation(out=vt[(b, e)][:], in_=mb[(b, e)][:], func=ACT.Relu, bias=biasf[:, j:j + 1], scale=1.0,
                                  accum_out=msum(b, e))
             if b >= 8:
-                rep[(b, e)] = work.tile([P, P], F32, name="rep%d_%d" % (b, e), tag="rep", bufs=10)
+                rep[(b, e)] = work.tile([P, P], F32, name="rep%d_%d" % (b, e), tag="rep", bufs=16)
                 if REP_ENG == "G" and b < 14:
                     nc.gpsimd.tensor_scalar(out=rep[(b, e)][:], in0=ones_f[:], scalar1=msum(b, e), scalar2=1.0 / ROWS, op0=ALU.mult, op1=ALU.mult)
                 else:
@@ -206,12 +206,12 @@ def tile_optimalnet_pa_kernel(tc, x, W1, b1, W2, b2, out_0, out_1, out_2):
 
         def adds(n):
             for i in range(n):
-                if added[0] == 0 and len(pending) >= 2:
-                    nc.vector.tensor_tensor(out=acc[:], in0=vt[pending[0]][:], in1=vt[pending[1]][:], op=ALU.add)
-                    added[0] = 2
-                elif 0 < added[0] < len(pending):
-                    nc.vector.tensor_tensor(out=acc[:], in0=acc[:], in1=vt[pending[added[0]]][:], op=ALU.add)
-                    added[0] = added[0] + 1
+                a = added[0]
+                if a < 2:
+                    nc.vector.tensor_tensor(out=acc[a][:], in0=vt[pending[a]][:], in1=vt[pending[a + 2]][:], op=ALU.add)
+                elif a < 14:
+                    nc.vector.tensor_tensor(out=acc[a % 2][:], in0=acc[a % 2][:], in1=vt[pending[a + 2]][:], op=ALU.add)
+                added[0] = min(a + 1, 14)
 
         def rg(g):
             gh[g] = work.tile([P, 2048], BF16, name="gh%d" % g, tag="gh", align_bytes=64)
@@ -223,7 +223,8 @@ def tile_optimalnet_pa_kernel(tc, x, W1, b1, W2, b2, out_0, out_1, out_2):
 
         def sh_vector():
             nc.vector.tensor_reduce(out=s1[:], in_=mp[0][:], axis=AX.X, op=ALU.add)
-            nc.vector.scalar_tensor_tensor(out=accf[:], in0=sxc[:], scalar=s1[:], in1=acc[:], op0=ALU.mult, op1=ALU.add)
+            nc.vector.scalar_tensor_tensor(out=accf[:], in0=sxc[:], scalar=s1[:], in1=acc[0][:], op0=ALU.mult, op1=ALU.add)
+            nc.vector.tensor_tensor(out=accf[:], in0=accf[:], in1=acc[1][:], op=ALU.add)
 
         def sh_rest():
             bank = psT.tile([P, 512], F32, name="shb", tag="T")
@@ -280,41 +281,53 @@ def tile_optimalnet_pa_kernel(tc, x, W1, b1, W2, b2, out_0, out_1, out_2):
         for b in range(1, NW - 2):
             load(b)
 
-        def txe(rt):
+        def txe(rt, engines):
             tx(rt)
-            ex(rt, 0, "V")
-            ex(rt, 1, "S")
-            qx(rt)
+            ex(rt, 0, engines[0])
+            ex(rt, 1, engines[1])
 
-        txe(0)
+        txe(0, "VS")
         warm_up(WARM1)
         bank = psT.tile([P, 512], F32, name="tbias", tag="T")
         nc.tensor.transpose(out=bank[:, 0:P], in_=bz[:].bitcast(F32), identity=ident[:])
         nc.vector.tensor_copy(out=bw[:], in_=bank[:, 0:16])
         nc.vector.tensor_copy(out=biasf[:], in_=bw[:].bitcast(BF16))
-        txe(1)
+        qx(0)
+        txe(1, "VS")
         load(NW - 2)
         sxmm(0)
         rsx(0)
-        txe(2)
+        qx(1)
+        txe(2, "VS")
         tw(0, (0, 1))
         ew(0, 0, "S")
         ew(0, 1, "V")
+        qx(2)
         qw(0, 0)
-        txe(3)
+        txe(3, "SV")
         load(NW - 1)
+        qx(3)
         sxmm(1)
         tw(0, (2, 3))
         load(NW)
         ew(0, 2, "S")
         ew(0, 3, "V")
-        qw(0, 1)
         rsx(1)
+        qw(0, 1)
 
         sh_step = [99]
         twd = [0]
         turned = [8]
-        for b in range(18):
+        def turn_next(b):
+            if b >= sh_step[0] + SH_DELAY and turned[0] <= min(15, b - (LAG if b < 14 else 1)):
+                to(turned[0])
+                em(turned[0])
+                if turned[0] == 15:
+                    nc.sync.dma_start(out=out_2.rearrange("(a n) -> a n", a=1), in_=m2b[0:1, :])
+                eo(turned[0])
+                turned[0] = turned[0] + 1
+
+        for b in range(20):
             prev = b - 1
             tlist = [t for t in range(twd[0] + 1, min(15, b + AH[min(b, 9)]) + 1)]
             if b == 0:
@@ -335,22 +348,13 @@ def tile_optimalnet_pa_kernel(tc, x, W1, b1, W2, b2, out_0, out_1, out_2):
                         rg(prev // 2)
                     if prev == 7:
                         qh(3)
-                    else:
-                        adds(ADDS_L1)
             if len(tlist) > 0:
                 for i in range(4):
                     ew(tlist[-1], i, EW_ENG[tlist[-1] // 8][i])
             if b == sh_step[0] + SH_DELAY:
                 sh_rest()
-            if b >= sh_step[0] + SH_DELAY:
-                for i in range(TO_PER_STEP):
-                    if turned[0] <= min(15, b - (LAG if b < 14 else 1)):
-                        to(turned[0])
-                        em(turned[0])
-                        if turned[0] == 15:
-                            nc.sync.dma_start(out=out_2.rearrange("(a n) -> a n", a=1), in_=m2b[0:1, :])
-                        eo(turned[0])
-                        turned[0] = turned[0] + 1
+            for i in range(TO_PER_STEP):
+                turn_next(b)
             if b == 9:
                 mout1()
             if b == 0:
@@ -375,6 +379,8 @@ def tile_optimalnet_pa_kernel(tc, x, W1, b1, W2, b2, out_0, out_1, out_2):
                 act(b, 0)
             for t in tlist:
                 qw(t)
+                if b == 8 and t == 9:
+                    adds(ADDS_8)
             if prev % 2 == 1 and 0 < prev < 7:
                 qh(prev // 2)
             if b == 0:
@@ -385,6 +391,6 @@ def tile_optimalnet_pa_kernel(tc, x, W1, b1, W2, b2, out_0, out_1, out_2):
                 hh(b, 0)
             if b >= 8 and sh_step[0] == 99:
                 adds(ADDS_L2)
-                if added[0] == 16:
+                if added[0] == 14:
                     sh_vector()
                     sh_step[0] = b

@@ -234,13 +234,12 @@ def tile_optimalnet_pa_kernel(tc, x, W1, b1, W2, b2, out_0, out_1, out_2):
 
         def to(b):
             for k in range(2):
-                bank = psT.tile([P, 512], F32, name="to%d_%d" % (b, k), tag="T")
-                for l in range(2):
-                    for e in range(2):
-                        rb = 2 * k + l
-                        nc.tensor.transpose(out=bank[:, (l * 2 + e) * P:(l * 2 + e + 1) * P], in_=vt[(b, e)][:, rb * P:(rb + 1) * P],
-                                            identity=ident[:])
-                tb[("o", b, k)] = bank
+                tb[("o", b, k)] = psT.tile([P, 512], F32, name="to%d_%d" % (b, k), tag="T")
+            for e in range(2):
+                for rb in range(4):
+                    k, l = rb // 2, rb % 2
+                    nc.tensor.transpose(out=tb[("o", b, k)][:, (l * 2 + e) * P:(l * 2 + e + 1) * P], in_=vt[(b, e)][:, rb * P:(rb + 1) * P],
+                                        identity=ident[:])
             bank = psT.tile([P, 512], F32, name="tr%d" % b, tag="T")
             for e in range(2):
                 nc.tensor.transpose(out=bank[:, e * P:(e + 1) * P], in_=rep[(b, e)][:], identity=ident[:])
@@ -301,17 +300,17 @@ def tile_optimalnet_pa_kernel(tc, x, W1, b1, W2, b2, out_0, out_1, out_2):
         txe(2, "VS")
         tw(0, (0, 1))
         ew(0, 0, "S")
-        ew(0, 1, "V")
+        ew(0, 1, "S")
         qx(2)
         qw(0, 0)
-        txe(3, "SV")
+        txe(3, "SS")
         load(NW - 1)
         qx(3)
         sxmm(1)
         tw(0, (2, 3))
         load(NW)
         ew(0, 2, "S")
-        ew(0, 3, "V")
+        ew(0, 3, "S")
         rsx(1)
         qw(0, 1)
 
@@ -350,7 +349,7 @@ def tile_optimalnet_pa_kernel(tc, x, W1, b1, W2, b2, out_0, out_1, out_2):
                         qh(3)
             if len(tlist) > 0:
                 for i in range(4):
-                    ew(tlist[-1], i, EW_ENG[tlist[-1] // 8][i])
+                    ew(tlist[-1], i, "SVSV"[i] if b == sh_step[0] + SH_DELAY else EW_ENG[tlist[-1] // 8][i])
             if b == sh_step[0] + SH_DELAY:
                 sh_rest()
             for i in range(TO_PER_STEP):

@@ -234,12 +234,13 @@ def tile_optimalnet_pa_kernel(tc, x, W1, b1, W2, b2, out_0, out_1, out_2):
 
         def to(b):
             for k in range(2):
-                tb[("o", b, k)] = psT.tile([P, 512], F32, name="to%d_%d" % (b, k), tag="T")
-            for e in range(2):
-                for rb in range(4):
-                    k, l = rb // 2, rb % 2
-                    nc.tensor.transpose(out=tb[("o", b, k)][:, (l * 2 + e) * P:(l * 2 + e + 1) * P], in_=vt[(b, e)][:, rb * P:(rb + 1) * P],
-                                        identity=ident[:])
+                bank = psT.tile([P, 512], F32, name="to%d_%d" % (b, k), tag="T")
+                for l in range(2):
+                    for e in range(2):
+                        rb = 2 * k + l
+                        nc.tensor.transpose(out=bank[:, (l * 2 + e) * P:(l * 2 + e + 1) * P], in_=vt[(b, e)][:, rb * P:(rb + 1) * P],
+                                            identity=ident[:])
+                tb[("o", b, k)] = bank
             bank = psT.tile([P, 512], F32, name="tr%d" % b, tag="T")
             for e in range(2):
                 nc.tensor.transpose(out=bank[:, e * P:(e + 1) * P], in_=rep[(b, e)][:], identity=ident[:])

@@ -41,7 +41,6 @@ def tile_optimalnet_pa_kernel(tc, x, W1, b1, W2, b2, out_0, out_1, out_2):
         work = ctx.enter_context(tc.tile_pool(name="work", bufs=2))
         psT = ctx.enter_context(tc.psum_pool(name="psT", bufs=6))
         psM = ctx.enter_context(tc.psum_pool(name="psM", bufs=2))
-        ctx.enter_context(tc.manual_schedule())
 
         def copy_on(eng, out, in_):
             if eng == "V":
@@ -301,17 +300,17 @@ def tile_optimalnet_pa_kernel(tc, x, W1, b1, W2, b2, out_0, out_1, out_2):
         txe(2, "VS")
         tw(0, (0, 1))
         ew(0, 0, "S")
-        ew(0, 1, "S")
+        ew(0, 1, "V")
         qx(2)
         qw(0, 0)
-        txe(3, "SS")
+        txe(3, "SV")
         load(NW - 1)
         qx(3)
         sxmm(1)
         tw(0, (2, 3))
         load(NW)
         ew(0, 2, "S")
-        ew(0, 3, "S")
+        ew(0, 3, "V")
         rsx(1)
         qw(0, 1)
 
@@ -350,7 +349,7 @@ def tile_optimalnet_pa_kernel(tc, x, W1, b1, W2, b2, out_0, out_1, out_2):
                         qh(3)
             if len(tlist) > 0:
                 for i in range(4):
-                    ew(tlist[-1], i, "SVSV"[i] if b == sh_step[0] + SH_DELAY else EW_ENG[tlist[-1] // 8][i])
+                    ew(tlist[-1], i, EW_ENG[tlist[-1] // 8][i])
             if b == sh_step[0] + SH_DELAY:
                 sh_rest()
             for i in range(TO_PER_STEP):

from contextlib import ExitStack

import concourse.mybir as mybir
from concourse.masks import make_identity

F32 = mybir.dt.float32
BF16 = mybir.dt.bfloat16
U32 = mybir.dt.uint32
U8 = mybir.dt.uint8
FP8X4 = mybir.dt.float8_e4m3fn_x4
ACT = mybir.ActivationFunctionType
ALU = mybir.AluOpType
AX = mybir.AxisListType

P = 128
ROWS = 512
C = 0.01 * 0.001 / 1
FLOPS = 2 * 2 * 512 * 2048 * 2048

NW = 6
EW_ENG = ["SSSS", "SSSS"]
EW0_ENG = "SVSV"
ADDS_L2 = 5
ADDS_8 = 3
LAG = 2
TO_PER_STEP = 2
SH_DELAY = 3
REP_ENG = "G"
NV = 18
WARM0 = 4
WARM1 = 2
AH = [1, 1, 1, 1, 1, 1, 1, 1, 1, 2]


def tile_optimalnet_pa_kernel(tc, x, W1, b1, W2, b2, out_0, out_1, out_2):
    nc = tc.nc
    with ExitStack() as ctx:
        const = ctx.enter_context(tc.tile_pool(name="const", bufs=1))
        win = ctx.enter_context(tc.tile_pool(name="win", bufs=NW))
        stage = ctx.enter_context(tc.tile_pool(name="stage", bufs=3))
        work = ctx.enter_context(tc.tile_pool(name="work", bufs=2))
        psT = ctx.enter_context(tc.psum_pool(name="psT", bufs=6))
        psM = ctx.enter_context(tc.psum_pool(name="psM", bufs=2))

        def copy_on(eng, out, in_):
            if eng == "V":
                nc.vector.tensor_copy(out=out, in_=in_)
            else:
                nc.scalar.copy(out=out, in_=in_)

        xt = [win.tile([P, 4096], BF16, name="x0", tag="w"), win.tile([P, 4096], BF16, name="x1", tag="w")]
        w0 = win.tile([P, 4096], BF16, name="w0", tag="w")

        def load_x(rt, lo=0, hi=2048):
            nc.sync.dma_start(out=xt[rt // 2][:, (rt % 2) * 2048 + lo:(rt % 2) * 2048 + hi], in_=x[rt * P:(rt + 1) * P, lo:hi])

        def load_w0(e):
            nc.sync.dma_start(out=w0[:, e * 2048:(e + 1) * 2048], in_=W1.rearrange("(c p e) k -> c p e k", p=P, e=2)[0][:, e, :])

        load_x(0, 0, 1024)
        load_x(0, 1024, 2048)
        ones_b = const.tile([P, 512], BF16, name="ones_b")
        nc.vector.memset(ones_b[:], 1.0)
        bz = const.tile([P, 256], BF16, name="bz")
        nc.vector.memset(bz[:], 0.0)
        nc.sync.dma_start(out=bz[0:8, :], in_=b1.rearrange("(c n) -> c n", n=256))
        nc.sync.dma_start(out=bz[8:16, :], in_=b2.rearrange("(c n) -> c n", n=256))
        load_x(1)
        load_x(2)
        load_w0(0)
        load_x(3)
        load_w0(1)
        ident = const.tile([P, P], F32, name="ident")
        make_identity(nc, ident[:])
        ones_f = const.tile([P, P], F32, name="ones_f")
        nc.vector.memset(ones_f[:], 1.0)
        mp = [const.tile([P, 256], F32, name="mp0"), const.tile([P, 16], F32, name="mp1")]
        nc.vector.memset(mp[0][:], 0.0)
        tabl = const.tile([P, 1], F32, name="tabl")
        nc.scalar.activation(out=tabl[:], in_=ones_f[:, 0:1], func=ACT.Relu)
        warm = psT.tile([P, 512], F32, name="warm", tag="T")

        def warm_up(n):
            for i in range(n):
                nc.tensor.matmul(out=warm[:], lhsT=ones_b[:, 0:P], rhs=ones_b[:], start=True, stop=True)

        warm_up(WARM0)

        gx = const.tile([P, 8192], BF16, name="gx", align_bytes=64)
        xc = const.tile([P, 2048], U32, name="xc", align_bytes=64)
        xsc = const.tile([P, 2048], U8, name="xsc", align_bytes=64)
        hc = const.tile([P, 2048], U32, name="hc", align_bytes=64)
        hsc = const.tile([P, 2048], U8, name="hsc", align_bytes=64)
        bw = const.tile([P, 16], F32, name="bw")
        biasf = const.tile([P, 32], F32, name="biasf")
        sxr = const.tile([P, ROWS], F32, name="sxr")
        sxc = const.tile([P, ROWS], F32, name="sxc")
        acc = [const.tile([P, ROWS], F32, name="acc0"), const.tile([P, ROWS], F32, name="acc1")]
        accf = const.tile([P, ROWS], F32, name="accf")
        shc = const.tile([P, 4], F32, name="shc")
        s1 = const.tile([P, 1], F32, name="s1")
        m2b = const.tile([P, 2048], F32, name="m2b")

        wsrc = [W1.rearrange("(c p e) k -> c p (e k)", p=P, e=2), W2.rearrange("(c p e) k -> c p (e k)", p=P, e=2)]
        wt, tb, gw, wc, ws, mb, vt, ob, hcn, gh, rep = {}, {}, {}, {}, {}, {}, {}, {}, {}, {}, {}

        def load(b):
            t = win.tile([P, 4096], BF16, name="w%d" % b, tag="w")
            nc.sync.dma_start(out=t[:], in_=wsrc[b // 8][b % 8])
            wt[b] = t

        def four_transposes(bank, src32, cols):
            for i in range(4):
                nc.tensor.transpose(out=bank[:, i * P:(i + 1) * P], in_=src32[:, cols[i]:cols[i] + P], identity=ident[:])

        def tx(rt):
            x32 = xt[rt // 2][:].bitcast(F32)
            for gp in range(2):
                bank = psT.tile([P, 512], F32, name="tx%d_%d" % (rt, gp), tag="T")
                four_transposes(bank, x32, [(rt % 2) * 1024 + (2 * gp + gl) * 256 + u * P for gl in range(2) for u in range(2)])
                tb[("x", rt, gp)] = bank

        def ex(rt, gp, eng):
            dst = gx[:].bitcast(F32).rearrange("p (g r u) -> p g r u", g=4, u=2)[:, 2 * gp:2 * gp + 2, rt * P:(rt + 1) * P, :]
            copy_on(eng, dst, tb[("x", rt, gp)][:].rearrange("p (g u r) -> p g r u", g=2, u=2))

        def qx(rt):
            for g in range(4):
                lo = g * 512 + rt * P
                nc.vector.quantize_mx(out=xc[:, lo:lo + P].bitcast(FP8X4), scales=xsc[:, lo:lo + P], in_=gx[:, 4 * lo:4 * (lo + P)])

        def sxmm(rt):
            bank = psT.tile([P, 512], F32, name="sx%d" % rt, tag="T")
            for g in range(4):
                nc.tensor.matmul(out=bank[:], lhsT=ones_b[:, 0:P], rhs=gx[:, g * 2048 + rt * 512:g * 2048 + (rt + 1) * 512],
                                 start=(g == 0), stop=(g == 3))
            tb[("s", rt)] = bank

        def rsx(rt):
            nc.vector.tensor_reduce(out=sxr[:, rt * P:(rt + 1) * P], in_=tb[("s", rt)][:].rearrange("p (r t) -> p r t", t=4),
                                    axis=AX.X, op=ALU.add)

        def tw(b, which=(0, 1, 2, 3)):
            w32 = wt[b][:].bitcast(F32)
            for i in which:
                e, gp = i // 2, i % 2
                bank = psT.tile([P, 512], F32, name="tw%d_%d" % (b, i), tag="T")
                four_transposes(bank, w32, [e * 1024 + (2 * gp + gl) * 256 + u * P for gl in range(2) for u in range(2)])
                tb[(b, i)] = bank

        def ew(b, i, eng):
            if i == 0:
                gw[b] = stage.tile([P, 4096], BF16, name="gw%d" % b, tag="gw", align_bytes=64)
            dst = gw[b][:].bitcast(F32)[:, i * 512:(i + 1) * 512].rearrange("p (g o u) -> p g o u", g=2, u=2)
            copy_on(eng, dst, tb[(b, i)][:].rearrange("p (g u o) -> p g o u", g=2, u=2))

        def qw(b, half=None):
            if half != 1:
                wc[b] = stage.tile([P, 1024], U32, name="wc%d" % b, tag="wc", align_bytes=64)
                ws[b] = stage.tile([P, 1024], U8, name="ws%d" % b, tag="ws", align_bytes=64)
            if half is None:
                nc.vector.quantize_mx(out=wc[b][:].bitcast(FP8X4), scales=ws[b][:], in_=gw[b][:])
            else:
                lo = half * 512
                nc.vector.quantize_mx(out=wc[b][:, lo:lo + 512].bitcast(FP8X4), scales=ws[b][:, lo:lo + 512], in_=gw[b][:, 4 * lo:4 * lo + 2048])

        def mm(b, es=(0, 1), gs=(0, 1, 2, 3)):
            rc, rs = (xc, xsc) if b < 8 else (hc, hsc)
            for e in es:
                if gs[0] == 0:
                    mb[(b, e)] = psM.tile([P, 512], F32, name="m%d_%d" % (b, e), tag="M")
            seq = [(e, g) for e in es for g in gs]
            for e, g in seq:
                lo = (e * 4 + g) * P
                nc.tensor.matmul_mx(out=mb[(b, e)][:], lhsT=wc[b][:, lo:lo + P].bitcast(FP8X4), lhsT_scale=ws[b][:, lo:lo + P],
                                    rhs=rc[:, g * 512:(g + 1) * 512].bitcast(FP8X4), rhs_scale=rs[:, g * 512:(g + 1) * 512],
                                    start=(g == 0), stop=(g == 3))

        def msum(b, e):
            col = e * P + b if b < 8 else (b - 8) * 2 + e
            return mp[b // 8][:, col:col + 1]

        def act(b, e):
            j = (b // 8) * 16 + (b % 8) * 2 + e
            vt[(b, e)] = work.tile([P, ROWS], F32, name="v%d_%d" % (b, e), tag="v", bufs=NV)
            nc.scalar.activation(out=vt[(b, e)][:], in_=mb[(b, e)][:], func=ACT.Relu, bias=biasf[:, j:j + 1], scale=1.0,
                                 accum_out=msum(b, e))
            if b >= 8:
                rep[(b, e)] = work.tile([P, P], F32, name="rep%d_%d" % (b, e), tag="rep", bufs=16)
                if REP_ENG == "G" and b < 14:
                    nc.gpsimd.tensor_scalar(out=rep[(b, e)][:], in0=ones_f[:], scalar1=msum(b, e), scalar2=1.0 / ROWS, op0=ALU.mult, op1=ALU.mult)
                else:
                    nc.vector.tensor_scalar(out=rep[(b, e)][:], in0=ones_f[:], scalar1=msum(b, e), scalar2=1.0 / ROWS, op0=ALU.mult, op1=ALU.mult)

        pending = []
        added = [0]

        def hh(b, e):
            g, t = b // 2, 2 * (b % 2) + e
            if t == 0:
                hcn[g] = work.tile([P, 2048], BF16, name="hcn%d" % g, tag="hcn")
            nc.vector.scalar_tensor_tensor(out=hcn[g][:, t * ROWS:(t + 1) * ROWS], in0=sxc[:], scalar=msum(b, e), in1=vt[(b, e)][:],
                                           op0=ALU.mult, op1=ALU.add)
            pending.append((b, e))

        def adds(n):
            for i in range(n):
                a = added[0]
                if a < 2:
                    nc.vector.tensor_tensor(out=acc[a][:], in0=vt[pending[a]][:], in1=vt[pending[a + 2]][:], op=ALU.add)
                elif a < 14:
                    nc.vector.tensor_tensor(out=acc[a % 2][:], in0=acc[a % 2][:], in1=vt[pending[a + 2]][:], op=ALU.add)
                added[0] = min(a + 1, 14)

        def rg(g):
            gh[g] = work.tile([P, 2048], BF16, name="gh%d" % g, tag="gh", align_bytes=64)
            nc.vector.tensor_copy(out=gh[g][:].rearrange("p (c i t) -> p c t i", i=4, t=4),
                                  in_=hcn[g][:].rearrange("p (t c i) -> p c t i", t=4, i=4))

        def qh(g):
            nc.vector.quantize_mx(out=hc[:, g * 512:(g + 1) * 512].bitcast(FP8X4), scales=hsc[:, g * 512:(g + 1) * 512], in_=gh[g][:])

        def sh_vector():
            nc.vector.tensor_reduce(out=s1[:], in_=mp[0][:], axis=AX.X, op=ALU.add)
            nc.vector.scalar_tensor_tensor(out=accf[:], in0=sxc[:], scalar=s1[:], in1=acc[0][:], op0=ALU.mult, op1=ALU.add)
            nc.vector.tensor_tensor(out=accf[:], in0=accf[:], in1=acc[1][:], op=ALU.add)

        def sh_rest():
            bank = psT.tile([P, 512], F32, name="shb", tag="T")
            for rb in range(4):
                nc.tensor.matmul(out=bank[:, rb * 32:(rb + 1) * 32], lhsT=accf[:, rb * P:(rb + 1) * P], rhs=ones_f[:, 0:32], start=True, stop=True)
            nc.scalar.mul(out=shc[:], in_=bank[:, 0:P].rearrange("p (b n) -> p b n", n=32)[:, :, 0], mul=C)

        def to(b):
            for k in range(2):
                bank = psT.tile([P, 512], F32, name="to%d_%d" % (b, k), tag="T")
                for l in range(2):
                    for e in range(2):
                        rb = 2 * k + l
                        nc.tensor.transpose(out=bank[:, (l * 2 + e) * P:(l * 2 + e + 1) * P], in_=vt[(b, e)][:, rb * P:(rb + 1) * P],
                                            identity=ident[:])
                tb[("o", b, k)] = bank
            bank = psT.tile([P, 512], F32, name="tr%d" % b, tag="T")
            for e in range(2):
                nc.tensor.transpose(out=bank[:, e * P:(e + 1) * P], in_=rep[(b, e)][:], identity=ident[:])
            tb[("r", b)] = bank

        def em(b):
            c = b - 8
            nc.scalar.copy(out=m2b[:, c * 256:(c + 1) * 256].rearrange("r (p e) -> r p e", e=2),
                           in_=tb[("r", b)][:, 0:256].rearrange("r (e p) -> r p e", e=2))

        def eo(b):
            c = b - 8
            ob[b] = work.tile([P, 1024], F32, name="o%d" % b, tag="o", bufs=3)
            for rb in range(4):
                k, l = rb // 2, rb % 2
                nc.vector.scalar_tensor_tensor(out=ob[b][:, rb * 256:(rb + 1) * 256].rearrange("r (p e) -> r p e", e=2),
                                               in0=m2b[:, c * 256:(c + 1) * 256].rearrange("r (p e) -> r p e", e=2),
                                               scalar=shc[:, rb:rb + 1],
                                               in1=tb[("o", b, k)][:, l * 256:(l + 1) * 256].rearrange("r (e p) -> r p e", e=2),
                                               op0=ALU.mult, op1=ALU.add)
                if b == 15 and rb % 2 == 1:
                    nc.sync.dma_start(out=out_0.rearrange("(k r) o -> r k o", r=P)[:, rb - 1:rb + 1, c * 256:(c + 1) * 256],
                                      in_=ob[b][:].rearrange("r (k o) -> r k o", k=4)[:, rb - 1:rb + 1, :])
            if b < 15:
                nc.sync.dma_start(out=out_0.rearrange("(k r) o -> r k o", r=P)[:, :, c * 256:(c + 1) * 256],
                                  in_=ob[b][:].rearrange("r (k o) -> r k o", k=4))

        def mout1():
            bank = psT.tile([P, 512], F32, name="mo", tag="T")
            for e in range(2):
                nc.tensor.transpose(out=bank[:, e * P:(e + 1) * P], in_=mp[0][:, e * P:(e + 1) * P], identity=ident[:])
            ms = work.tile([P, 256], F32, name="ms", tag="ms", bufs=1)
            nc.scalar.activation(out=ms[:].rearrange("c (p e) -> c p e", e=2), in_=bank[:, 0:256].rearrange("c (e p) -> c p e", e=2),
                                 func=ACT.Copy, scale=1.0 / ROWS)
            nc.sync.dma_start(out=out_1.rearrange("(c n) -> c n", n=256), in_=ms[0:8, :])

        wt[0] = w0
        for b in range(1, NW - 2):
            load(b)

        def txe(rt, engines):
            tx(rt)
            ex(rt, 0, engines[0])
            ex(rt, 1, engines[1])

        txe(0, "VS")
        warm_up(WARM1)
        bank = psT.tile([P, 512], F32, name="tbias", tag="T")
        nc.tensor.transpose(out=bank[:, 0:P], in_=bz[:].bitcast(F32), identity=ident[:])
        nc.vector.tensor_copy(out=bw[:], in_=bank[:, 0:16])
        nc.vector.tensor_copy(out=biasf[:], in_=bw[:].bitcast(BF16))
        qx(0)
        txe(1, "VS")
        load(NW - 2)
        sxmm(0)
        rsx(0)
        qx(1)
        txe(2, "VS")
        tw(0, (0, 1))
        ew(0, 0, "S")
        ew(0, 1, "V")
        qx(2)
        qw(0, 0)
        txe(3, "SV")
        load(NW - 1)
        qx(3)
        sxmm(1)
        tw(0, (2, 3))
        load(NW)
        ew(0, 2, "S")
        ew(0, 3, "V")
        rsx(1)
        qw(0, 1)

        sh_step = [99]
        twd = [0]
        turned = [8]
        def turn_next(b):
            if b >= sh_step[0] + SH_DELAY and turned[0] <= min(15, b - (LAG if b < 14 else 1)):
                to(turned[0])
                em(turned[0])
                if turned[0] == 15:
                    nc.sync.dma_start(out=out_2.rearrange("(a n) -> a n", a=1), in_=m2b[0:1, :])
                eo(turned[0])
                turned[0] = turned[0] + 1

        for b in range(20):
            prev = b - 1
            tlist = [t for t in range(twd[0] + 1, min(15, b + AH[min(b, 9)]) + 1)]
            if b == 0:
                mm(0, (0,))
            for t in tlist:
                tw(t)
                twd[0] = t
                if t + NW <= 15:
                    load(t + NW)
                if t != tlist[-1]:
                    for i in range(4):
                        ew(t, i, "SVSV"[i])
            if 0 <= prev <= 15:
                act(prev, 1)
                if prev <= 7:
                    hh(prev, 1)
                    if prev % 2 == 1:
                        rg(prev // 2)
                    if prev == 7:
                        qh(3)
            if len(tlist) > 0:
                for i in range(4):
                    ew(tlist[-1], i, EW_ENG[tlist[-1] // 8][i])
            if b == sh_step[0] + SH_DELAY:
                sh_rest()
            for i in range(TO_PER_STEP):
                turn_next(b)
            if b == 9:
                mout1()
            if b == 0:
                act(0, 0)
                mm(0, (1,))
                sxmm(2)
                sxmm(3)
            elif b == 8:
                mm(8, (0, 1), (0, 1, 2))
                tx_ = twd[0] + 1
                tw(tx_)
                twd[0] = tx_
                if tx_ + NW <= 15:
                    load(tx_ + NW)
                for i in range(4):
                    ew(tx_, i, "SSSS"[i])
                tlist.append(tx_)
                mm(8, (0, 1), (3,))
                act(8, 0)
            elif b <= 15:
                mm(b)
                act(b, 0)
            for t in tlist:
                qw(t)
                if b == 8 and t == 9:
                    adds(ADDS_8)
            if prev % 2 == 1 and 0 < prev < 7:
                qh(prev // 2)
            if b == 0:
                rsx(2)
                rsx(3)
                nc.vector.tensor_scalar(out=sxc[:], in0=sxr[:], scalar1=C / ROWS, scalar2=None, op0=ALU.mult)
            if b <= 7:
                hh(b, 0)
            if b >= 8 and sh_step[0] == 99:
                adds(ADDS_L2)
                if added[0] == 14:
                    sh_vector()
                    sh_step[0] = b
